import numpy as np
import ml_dtypes

BF16 = ml_dtypes.bfloat16


def bf(x):
    return np.asarray(x, np.float32).astype(BF16)


def f32(x):
    return np.asarray(x, np.float32)


def f64(x):
    return np.asarray(x).astype(np.float64)


def striped(idx):
    return np.tile(idx.reshape(-1, 16).T, (8, 1))


C, S, N, HID, HD, HALF, NKV = 256, 1024, 128, 256, 128, 64, 2
EPS = 1e-6


def setup_inputs():
    ang = np.random.uniform(0.0, 2.0 * np.pi, (HALF, N))
    return {"base": f32(0.5 * np.random.standard_normal((C, S))), "h": bf(np.random.standard_normal((HID, N))), "wk": bf(np.random.standard_normal((HID, C)) / np.sqrt(HID)), "k_norm_w": f32(1.0 + 0.1 * np.random.standard_normal((HD, 1))), "cs": f32(np.concatenate([np.cos(ang), np.sin(ang)], axis=0)), "offs": striped(np.random.permutation(S)[:N])}


def reference(base, h, wk, k_norm_w, cs, offs):
    idx = offs[:16].T.reshape(-1)
    k = (f64(wk).T @ f64(h)).reshape(NKV, HD, N)
    kn = k / np.sqrt(np.mean(k * k, axis=1, keepdims=True) + EPS) * f64(k_norm_w)[None]
    cos = f64(cs)[:HALF][None]
    sin = f64(cs)[HALF:][None]
    k1 = kn[:, :HALF]
    k2 = kn[:, HALF:]
    rot = np.concatenate([k1 * cos + (-(k2 * sin)), k2 * cos + k1 * sin], axis=1).reshape(C, N)
    out = f64(base).copy()
    out[:, idx] = rot
    return out

@@ -1,0 +1,100 @@
+import concourse.mybir as mybir
+
+F32 = mybir.dt.float32
+BF16 = mybir.dt.bfloat16
+U16 = mybir.dt.uint16
+MULT = mybir.AluOpType.mult
+ADD = mybir.AluOpType.add
+ACT = mybir.ActivationFunctionType
+
+P = 128
+HEADS = 2
+HALF = 64
+TOKENS = 128
+SLOTS = 1024
+HIDDEN_BLOCKS = 2
+EPS = 1e-6
+
+FLOPS = 2 * (HIDDEN_BLOCKS * P) * (HEADS * P) * TOKENS
+
+
+def tile_selfattention_s_kernel(tc, base, h, wk, k_norm_w, cs, offs, out):
+    nc = tc.nc
+    with (
+        tc.tile_pool(name="held", bufs=1) as held,
+        tc.tile_pool(name="work", bufs=2) as work,
+        tc.psum_pool(name="psum", bufs=2) as psum,
+    ):
+        h_sb = held.tile([P, HIDDEN_BLOCKS, TOKENS], BF16, name="h_sb")
+        nc.sync.dma_start(h_sb[:], h.rearrange("(kb p) j -> p kb j", p=P))
+        wk_sb = held.tile([P, HIDDEN_BLOCKS, HEADS * P], BF16, name="wk_sb")
+        nc.scalar.dma_start(wk_sb[:], wk.rearrange("(kb p) c -> p kb c", p=P))
+        offsets = held.tile([P, TOKENS // 16], U16, name="offsets")
+        nc.sync.dma_start(offsets[:], offs)
+
+        cos2 = held.tile([P, TOKENS], F32, name="cos2")
+        sin2 = held.tile([P, TOKENS], F32, name="sin2")
+        for half in range(2):
+            rows = slice(half * HALF, (half + 1) * HALF)
+            nc.sync.dma_start(cos2[rows, :], cs[0:HALF, :])
+            nc.scalar.dma_start(sin2[rows, :], cs[HALF:P, :])
+        gain = held.tile([P, 1], F32, name="gain")
+        partner_gain = held.tile([P, 1], F32, name="partner_gain")
+        nc.sync.dma_start(gain[:], k_norm_w)
+        nc.scalar.dma_start(partner_gain[0:HALF, :], k_norm_w[HALF:P, :])
+        nc.scalar.dma_start(partner_gain[HALF:P, :], k_norm_w[0:HALF, :])
+
+        windows = [held.tile([P, SLOTS], F32, name=f"window{t}") for t in range(HEADS)]
+        nc.sync.dma_start(windows[0][:], base[0:P, :])
+        nc.scalar.dma_start(windows[1][:], base[P : 2 * P, :])
+
+        ones = held.tile([P, P], BF16, name="ones")
+        nc.gpsimd.memset(ones[:], 1.0)
+        eps = held.tile([P, 1], F32, name="eps")
+        nc.gpsimd.memset(eps[:], EPS)
+
+        wk_partner = held.tile([P, HIDDEN_BLOCKS, HEADS * P], BF16, name="wk_partner")
+        halves = wk_sb[:].rearrange("p kb (t half e) -> p (kb t) half e", half=2, e=HALF)
+        partner_halves = wk_partner[:].rearrange("p kb (t half e) -> p (kb t) half e", half=2, e=HALF)
+        nc.vector.tensor_copy(partner_halves[:, :, 0, :], halves[:, :, 1, :])
+        nc.vector.tensor_copy(partner_halves[:, :, 1, :], halves[:, :, 0, :])
+
+        nc.vector.tensor_scalar_mul(partner_gain[0:HALF, :], partner_gain[0:HALF, :], -1.0)
+        cos_gain = held.tile([P, TOKENS], F32, name="cos_gain")
+        sin_gain = held.tile([P, TOKENS], F32, name="sin_gain")
+        nc.vector.tensor_scalar_mul(cos_gain[:], cos2[:], gain[:, 0:1])
+        nc.vector.tensor_scalar_mul(sin_gain[:], sin2[:], partner_gain[:, 0:1])
+
+        for t in range(HEADS):
+            head_cols = slice(t * P, (t + 1) * P)
+
+            k_ps = psum.tile([P, TOKENS], F32, name="k_ps")
+            for kb in range(HIDDEN_BLOCKS):
+                nc.tensor.matmul(
+                    k_ps[:], wk_sb[:, kb, head_cols], h_sb[:, kb, :],
+                    start=(kb == 0), stop=(kb == HIDDEN_BLOCKS - 1),
+                )
+            partner_ps = psum.tile([P, TOKENS], F32, name="partner_ps")
+            for kb in range(HIDDEN_BLOCKS):
+                nc.tensor.matmul(
+                    partner_ps[:], wk_partner[:, kb, head_cols], h_sb[:, kb, :],
+                    start=(kb == 0), stop=(kb == HIDDEN_BLOCKS - 1),
+                )
+
+            squares = work.tile([P, TOKENS], BF16, name="squares")
+            nc.scalar.activation(squares[:], k_ps[:], ACT.Square)
+            sum_ps = psum.tile([P, TOKENS], F32, name="sum_ps")
+            nc.tensor.matmul(sum_ps[:], ones[:], squares[:], start=True, stop=True)
+            r = work.tile([P, TOKENS], F32, name="r")
+            nc.scalar.activation(r[:], sum_ps[:], ACT.Abs_reciprocal_sqrt, bias=eps[:, 0:1], scale=1.0 / P)
+
+            straight = work.tile([P, TOKENS], F32, name="straight")
+            crossed = work.tile([P, TOKENS], F32, name="crossed")
+            nc.vector.tensor_tensor(straight[:], k_ps[:], cos_gain[:], MULT)
+            nc.vector.tensor_tensor(crossed[:], partner_ps[:], sin_gain[:], MULT)
+            nc.vector.tensor_tensor(straight[:], straight[:], r[:], MULT)
+            nc.vector.tensor_tensor(crossed[:], crossed[:], r[:], MULT)
+
+            nc.vector.tensor_tensor(windows[t][:].indirect(offsets[:]), straight[:], crossed[:], ADD)
+            store_queue = nc.sync if t == 0 else nc.scalar
+            store_queue.dma_start(out[head_cols, :], windows[t][:])

@@ -29,29 +29,30 @@ def tile_selfattention_s_kernel(tc, base, h, wk, k_norm_w, cs, offs, out):
         nc.sync.dma_start(h_sb[:], h.rearrange("(kb p) j -> p kb j", p=P))
         wk_sb = held.tile([P, HIDDEN_BLOCKS, HEADS * P], BF16, name="wk_sb")
         nc.scalar.dma_start(wk_sb[:], wk.rearrange("(kb p) c -> p kb c", p=P))
-        offsets = held.tile([P, TOKENS // 16], U16, name="offsets")
-        nc.sync.dma_start(offsets[:], offs)
 
-        cos2 = held.tile([P, TOKENS], F32, name="cos2")
-        sin2 = held.tile([P, TOKENS], F32, name="sin2")
+        windows = [held.tile([P, SLOTS], F32, name=f"window{t}") for t in range(HEADS)]
+        for t in range(HEADS):
+            nc.gpsimd.dma_start(windows[t][:], base[t * P : (t + 1) * P, :])
+
+        cos_sin = held.tile([P, 2, TOKENS], F32, name="cos_sin")
         for half in range(2):
-            rows = slice(half * HALF, (half + 1) * HALF)
-            nc.sync.dma_start(cos2[rows, :], cs[0:HALF, :])
-            nc.scalar.dma_start(sin2[rows, :], cs[HALF:P, :])
+            nc.sync.dma_start(
+                cos_sin[half * HALF : (half + 1) * HALF, :, :], cs.rearrange("(f e) j -> e f j", e=HALF)
+            )
         gain = held.tile([P, 1], F32, name="gain")
         partner_gain = held.tile([P, 1], F32, name="partner_gain")
         nc.sync.dma_start(gain[:], k_norm_w)
-        nc.scalar.dma_start(partner_gain[0:HALF, :], k_norm_w[HALF:P, :])
-        nc.scalar.dma_start(partner_gain[HALF:P, :], k_norm_w[0:HALF, :])
-
-        windows = [held.tile([P, SLOTS], F32, name=f"window{t}") for t in range(HEADS)]
-        nc.sync.dma_start(windows[0][:], base[0:P, :])
-        nc.scalar.dma_start(windows[1][:], base[P : 2 * P, :])
+        nc.sync.dma_start(partner_gain[0:HALF, :], k_norm_w[HALF:P, :])
+        nc.sync.dma_start(partner_gain[HALF:P, :], k_norm_w[0:HALF, :])
+        offsets = held.tile([P, TOKENS // 16], U16, name="offsets")
+        nc.sync.dma_start(offsets[:], offs)
 
         ones = held.tile([P, P], BF16, name="ones")
-        nc.gpsimd.memset(ones[:], 1.0)
+        nc.vector.memset(ones[:], 1.0)
         eps = held.tile([P, 1], F32, name="eps")
-        nc.gpsimd.memset(eps[:], EPS)
+        nc.vector.memset(eps[:], EPS)
+        table_warmer = held.tile([P, 1], F32, name="table_warmer")
+        nc.scalar.activation(table_warmer[:], eps[:], ACT.Abs_reciprocal_sqrt)
 
         wk_partner = held.tile([P, HIDDEN_BLOCKS, HEADS * P], BF16, name="wk_partner")
         halves = wk_sb[:].rearrange("p kb (t half e) -> p (kb t) half e", half=2, e=HALF)
@@ -62,8 +63,8 @@ def tile_selfattention_s_kernel(tc, base, h, wk, k_norm_w, cs, offs, out):
         nc.vector.tensor_scalar_mul(partner_gain[0:HALF, :], partner_gain[0:HALF, :], -1.0)
         cos_gain = held.tile([P, TOKENS], F32, name="cos_gain")
         sin_gain = held.tile([P, TOKENS], F32, name="sin_gain")
-        nc.vector.tensor_scalar_mul(cos_gain[:], cos2[:], gain[:, 0:1])
-        nc.vector.tensor_scalar_mul(sin_gain[:], sin2[:], partner_gain[:, 0:1])
+        nc.vector.tensor_scalar_mul(cos_gain[:], cos_sin[:, 0, :], gain[:, 0:1])
+        nc.vector.tensor_scalar_mul(sin_gain[:], cos_sin[:, 1, :], partner_gain[:, 0:1])
 
         for t in range(HEADS):
             head_cols = slice(t * P, (t + 1) * P)

@@ -24,28 +24,29 @@ def tile_selfattention_s_kernel(tc, base, h, wk, k_norm_w, cs, offs, out):
         tc.tile_pool(name="held", bufs=1) as held,
         tc.tile_pool(name="work", bufs=2) as work,
         tc.psum_pool(name="psum", bufs=2) as psum,
+        tc.psum_pool(name="psum_held", bufs=1) as psum_held,
     ):
         h_sb = held.tile([P, HIDDEN_BLOCKS, TOKENS], BF16, name="h_sb")
         nc.sync.dma_start(h_sb[:], h.rearrange("(kb p) j -> p kb j", p=P))
         wk_sb = held.tile([P, HIDDEN_BLOCKS, HEADS * P], BF16, name="wk_sb")
         nc.scalar.dma_start(wk_sb[:], wk.rearrange("(kb p) c -> p kb c", p=P))
 
-        windows = [held.tile([P, SLOTS], F32, name=f"window{t}") for t in range(HEADS)]
-        for t in range(HEADS):
-            nc.gpsimd.dma_start(windows[t][:], base[t * P : (t + 1) * P, :])
-
+        gain_row = held.tile([1, 2 * P], F32, name="gain_row")
+        nc.sync.dma_start(
+            gain_row[:].rearrange("o (twice d) -> o twice d", twice=2),
+            k_norm_w.rearrange("d o -> o d").unsqueeze(1).to_broadcast([1, 2, P]),
+        )
         cos_sin = held.tile([P, 2, TOKENS], F32, name="cos_sin")
         for half in range(2):
             nc.sync.dma_start(
                 cos_sin[half * HALF : (half + 1) * HALF, :, :], cs.rearrange("(f e) j -> e f j", e=HALF)
             )
-        gain = held.tile([P, 1], F32, name="gain")
-        partner_gain = held.tile([P, 1], F32, name="partner_gain")
-        nc.sync.dma_start(gain[:], k_norm_w)
-        nc.sync.dma_start(partner_gain[0:HALF, :], k_norm_w[HALF:P, :])
-        nc.sync.dma_start(partner_gain[HALF:P, :], k_norm_w[0:HALF, :])
         offsets = held.tile([P, TOKENS // 16], U16, name="offsets")
         nc.sync.dma_start(offsets[:], offs)
+
+        windows = [held.tile([P, SLOTS], F32, name=f"window{t}") for t in range(HEADS)]
+        nc.scalar.dma_start(windows[1][:], base[P : 2 * P, :])
+        nc.sync.dma_start(windows[0][:], base[0:P, :])
 
         ones = held.tile([P, P], BF16, name="ones")
         nc.vector.memset(ones[:], 1.0)
@@ -60,11 +61,17 @@ def tile_selfattention_s_kernel(tc, base, h, wk, k_norm_w, cs, offs, out):
         nc.vector.tensor_copy(partner_halves[:, :, 0, :], halves[:, :, 1, :])
         nc.vector.tensor_copy(partner_halves[:, :, 1, :], halves[:, :, 0, :])
 
-        nc.vector.tensor_scalar_mul(partner_gain[0:HALF, :], partner_gain[0:HALF, :], -1.0)
+        one = held.tile([1, 1], F32, name="one")
+        nc.vector.memset(one[:], 1.0)
+        gains_ps = psum_held.tile([P, 2], F32, name="gains_ps")
+        nc.tensor.matmul(gains_ps[:, 0:1], gain_row[:, 0:P], one[:], start=True, stop=True)
+        nc.tensor.matmul(gains_ps[:, 1:2], gain_row[:, HALF : HALF + P], one[:], start=True, stop=True)
+
+        nc.vector.tensor_scalar_mul(cos_sin[0:HALF, 1, :], cos_sin[0:HALF, 1, :], -1.0)
         cos_gain = held.tile([P, TOKENS], F32, name="cos_gain")
         sin_gain = held.tile([P, TOKENS], F32, name="sin_gain")
-        nc.vector.tensor_scalar_mul(cos_gain[:], cos_sin[:, 0, :], gain[:, 0:1])
-        nc.vector.tensor_scalar_mul(sin_gain[:], cos_sin[:, 1, :], partner_gain[:, 0:1])
+        nc.vector.tensor_scalar_mul(cos_gain[:], cos_sin[:, 0, :], gains_ps[:, 0:1])
+        nc.vector.tensor_scalar_mul(sin_gain[:], cos_sin[:, 1, :], gains_ps[:, 1:2])
 
         for t in range(HEADS):
             head_cols = slice(t * P, (t + 1) * P)

@@ -22,31 +22,29 @@ def tile_selfattention_s_kernel(tc, base, h, wk, k_norm_w, cs, offs, out):
     nc = tc.nc
     with (
         tc.tile_pool(name="held", bufs=1) as held,
-        tc.tile_pool(name="work", bufs=2) as work,
-        tc.psum_pool(name="psum", bufs=2) as psum,
-        tc.psum_pool(name="psum_held", bufs=1) as psum_held,
+        tc.psum_pool(name="psum", bufs=1) as psum,
     ):
         h_sb = held.tile([P, HIDDEN_BLOCKS, TOKENS], BF16, name="h_sb")
-        nc.sync.dma_start(h_sb[:], h.rearrange("(kb p) j -> p kb j", p=P))
+        nc.sync.dma_start(h_sb[:], h.rearrange("(p kb) j -> p kb j", kb=HIDDEN_BLOCKS))
         wk_sb = held.tile([P, HIDDEN_BLOCKS, HEADS * P], BF16, name="wk_sb")
-        nc.scalar.dma_start(wk_sb[:], wk.rearrange("(kb p) c -> p kb c", p=P))
+        nc.scalar.dma_start(wk_sb[:], wk.rearrange("(p kb) c -> p kb c", kb=HIDDEN_BLOCKS))
 
-        gain_row = held.tile([1, 2 * P], F32, name="gain_row")
-        nc.sync.dma_start(
-            gain_row[:].rearrange("o (twice d) -> o twice d", twice=2),
-            k_norm_w.rearrange("d o -> o d").unsqueeze(1).to_broadcast([1, 2, P]),
-        )
+        windows = [held.tile([P, SLOTS], F32, name=f"window{t}") for t in range(HEADS)]
+        for t in range(HEADS):
+            nc.gpsimd.dma_start(windows[t][:], base[t * P : (t + 1) * P, :])
+
         cos_sin = held.tile([P, 2, TOKENS], F32, name="cos_sin")
         for half in range(2):
             nc.sync.dma_start(
                 cos_sin[half * HALF : (half + 1) * HALF, :, :], cs.rearrange("(f e) j -> e f j", e=HALF)
             )
+        gain = held.tile([P, 1], F32, name="gain")
+        partner_gain = held.tile([P, 1], F32, name="partner_gain")
+        nc.sync.dma_start(gain[:], k_norm_w)
+        nc.sync.dma_start(partner_gain[0:HALF, :], k_norm_w[HALF:P, :])
+        nc.sync.dma_start(partner_gain[HALF:P, :], k_norm_w[0:HALF, :])
         offsets = held.tile([P, TOKENS // 16], U16, name="offsets")
         nc.sync.dma_start(offsets[:], offs)
-
-        windows = [held.tile([P, SLOTS], F32, name=f"window{t}") for t in range(HEADS)]
-        nc.scalar.dma_start(windows[1][:], base[P : 2 * P, :])
-        nc.sync.dma_start(windows[0][:], base[0:P, :])
 
         ones = held.tile([P, P], BF16, name="ones")
         nc.vector.memset(ones[:], 1.0)
@@ -55,54 +53,51 @@ def tile_selfattention_s_kernel(tc, base, h, wk, k_norm_w, cs, offs, out):
         table_warmer = held.tile([P, 1], F32, name="table_warmer")
         nc.scalar.activation(table_warmer[:], eps[:], ACT.Abs_reciprocal_sqrt)
 
+        k_ps = [psum.tile([P, TOKENS], F32, name=f"k_ps{t}") for t in range(HEADS)]
+        squares = [held.tile([P, TOKENS], BF16, name=f"squares{t}") for t in range(HEADS)]
+        for t in range(HEADS):
+            for kb in range(HIDDEN_BLOCKS):
+                nc.tensor.matmul(
+                    k_ps[t][:], wk_sb[:, kb, t * P : (t + 1) * P], h_sb[:, kb, :],
+                    start=(kb == 0), stop=(kb == HIDDEN_BLOCKS - 1),
+                )
+            nc.scalar.activation(squares[t][:], k_ps[t][:], ACT.Square)
+
         wk_partner = held.tile([P, HIDDEN_BLOCKS, HEADS * P], BF16, name="wk_partner")
         halves = wk_sb[:].rearrange("p kb (t half e) -> p (kb t) half e", half=2, e=HALF)
         partner_halves = wk_partner[:].rearrange("p kb (t half e) -> p (kb t) half e", half=2, e=HALF)
         nc.vector.tensor_copy(partner_halves[:, :, 0, :], halves[:, :, 1, :])
         nc.vector.tensor_copy(partner_halves[:, :, 1, :], halves[:, :, 0, :])
+        partner_ps = [psum.tile([P, TOKENS], F32, name=f"partner_ps{t}") for t in range(HEADS)]
+        for t in range(HEADS):
+            for kb in range(HIDDEN_BLOCKS):
+                nc.tensor.matmul(
+                    partner_ps[t][:], wk_partner[:, kb, t * P : (t + 1) * P], h_sb[:, kb, :],
+                    start=(kb == 0), stop=(kb == HIDDEN_BLOCKS - 1),
+                )
 
-        one = held.tile([1, 1], F32, name="one")
-        nc.vector.memset(one[:], 1.0)
-        gains_ps = psum_held.tile([P, 2], F32, name="gains_ps")
-        nc.tensor.matmul(gains_ps[:, 0:1], gain_row[:, 0:P], one[:], start=True, stop=True)
-        nc.tensor.matmul(gains_ps[:, 1:2], gain_row[:, HALF : HALF + P], one[:], start=True, stop=True)
+        nc.vector.tensor_scalar_mul(partner_gain[0:HALF, :], partner_gain[0:HALF, :], -1.0)
 
-        nc.vector.tensor_scalar_mul(cos_sin[0:HALF, 1, :], cos_sin[0:HALF, 1, :], -1.0)
-        cos_gain = held.tile([P, TOKENS], F32, name="cos_gain")
-        sin_gain = held.tile([P, TOKENS], F32, name="sin_gain")
-        nc.vector.tensor_scalar_mul(cos_gain[:], cos_sin[:, 0, :], gains_ps[:, 0:1])
-        nc.vector.tensor_scalar_mul(sin_gain[:], cos_sin[:, 1, :], gains_ps[:, 1:2])
+        products = [held.tile([P, 2, TOKENS], F32, name=f"products{t}") for t in range(HEADS)]
+        for t in range(HEADS):
+            nc.vector.scalar_tensor_tensor(
+                products[t][:, 0, :], k_ps[t][:], gain[:, 0:1], cos_sin[:, 0, :], MULT, MULT
+            )
+            nc.vector.scalar_tensor_tensor(
+                products[t][:, 1, :], partner_ps[t][:], partner_gain[:, 0:1], cos_sin[:, 1, :], MULT, MULT
+            )
 
         for t in range(HEADS):
-            head_cols = slice(t * P, (t + 1) * P)
-
-            k_ps = psum.tile([P, TOKENS], F32, name="k_ps")
-            for kb in range(HIDDEN_BLOCKS):
-                nc.tensor.matmul(
-                    k_ps[:], wk_sb[:, kb, head_cols], h_sb[:, kb, :],
-                    start=(kb == 0), stop=(kb == HIDDEN_BLOCKS - 1),
-                )
-            partner_ps = psum.tile([P, TOKENS], F32, name="partner_ps")
-            for kb in range(HIDDEN_BLOCKS):
-                nc.tensor.matmul(
-                    partner_ps[:], wk_partner[:, kb, head_cols], h_sb[:, kb, :],
-                    start=(kb == 0), stop=(kb == HIDDEN_BLOCKS - 1),
-                )
-
-            squares = work.tile([P, TOKENS], BF16, name="squares")
-            nc.scalar.activation(squares[:], k_ps[:], ACT.Square)
-            sum_ps = psum.tile([P, TOKENS], F32, name="sum_ps")
-            nc.tensor.matmul(sum_ps[:], ones[:], squares[:], start=True, stop=True)
-            r = work.tile([P, TOKENS], F32, name="r")
+            sum_ps = psum.tile([P, TOKENS], F32, name=f"sum_ps{t}")
+            nc.tensor.matmul(sum_ps[:], ones[:], squares[t][:], start=True, stop=True)
+            r = held.tile([P, TOKENS], F32, name=f"r{t}")
             nc.scalar.activation(r[:], sum_ps[:], ACT.Abs_reciprocal_sqrt, bias=eps[:, 0:1], scale=1.0 / P)
 
-            straight = work.tile([P, TOKENS], F32, name="straight")
-            crossed = work.tile([P, TOKENS], F32, name="crossed")
-            nc.vector.tensor_tensor(straight[:], k_ps[:], cos_gain[:], MULT)
-            nc.vector.tensor_tensor(crossed[:], partner_ps[:], sin_gain[:], MULT)
-            nc.vector.tensor_tensor(straight[:], straight[:], r[:], MULT)
-            nc.vector.tensor_tensor(crossed[:], crossed[:], r[:], MULT)
-
-            nc.vector.tensor_tensor(windows[t][:].indirect(offsets[:]), straight[:], crossed[:], ADD)
+            nc.vector.tensor_tensor(
+                products[t][:], products[t][:], r[:].unsqueeze(1).to_broadcast([P, 2, TOKENS]), MULT
+            )
+            nc.vector.tensor_tensor(
+                windows[t][:].indirect(offsets[:]), products[t][:, 0, :], products[t][:, 1, :], ADD
+            )
             store_queue = nc.sync if t == 0 else nc.scalar
-            store_queue.dma_start(out[head_cols, :], windows[t][:])
+            store_queue.dma_start(out[t * P : (t + 1) * P, :], windows[t][:])

@@ -30,8 +30,7 @@ def tile_selfattention_s_kernel(tc, base, h, wk, k_norm_w, cs, offs, out):
         nc.scalar.dma_start(wk_sb[:], wk.rearrange("(p kb) c -> p kb c", kb=HIDDEN_BLOCKS))
 
         windows = [held.tile([P, SLOTS], F32, name=f"window{t}") for t in range(HEADS)]
-        for t in range(HEADS):
-            nc.gpsimd.dma_start(windows[t][:], base[t * P : (t + 1) * P, :])
+        nc.gpsimd.dma_start(windows[0][:], base[0:P, :])
 
         cos_sin = held.tile([P, 2, TOKENS], F32, name="cos_sin")
         for half in range(2):
@@ -45,6 +44,7 @@ def tile_selfattention_s_kernel(tc, base, h, wk, k_norm_w, cs, offs, out):
         nc.sync.dma_start(partner_gain[HALF:P, :], k_norm_w[0:HALF, :])
         offsets = held.tile([P, TOKENS // 16], U16, name="offsets")
         nc.sync.dma_start(offsets[:], offs)
+        nc.sync.dma_start(windows[1][:], base[P : 2 * P, :])
 
         ones = held.tile([P, P], BF16, name="ones")
         nc.vector.memset(ones[:], 1.0)

@@ -30,7 +30,6 @@ def tile_selfattention_s_kernel(tc, base, h, wk, k_norm_w, cs, offs, out):
         nc.scalar.dma_start(wk_sb[:], wk.rearrange("(p kb) c -> p kb c", kb=HIDDEN_BLOCKS))
 
         windows = [held.tile([P, SLOTS], F32, name=f"window{t}") for t in range(HEADS)]
-        nc.gpsimd.dma_start(windows[0][:], base[0:P, :])
 
         cos_sin = held.tile([P, 2, TOKENS], F32, name="cos_sin")
         for half in range(2):
@@ -42,6 +41,7 @@ def tile_selfattention_s_kernel(tc, base, h, wk, k_norm_w, cs, offs, out):
         nc.sync.dma_start(gain[:], k_norm_w)
         nc.sync.dma_start(partner_gain[0:HALF, :], k_norm_w[HALF:P, :])
         nc.sync.dma_start(partner_gain[HALF:P, :], k_norm_w[0:HALF, :])
+        nc.sync.dma_start(windows[0][:], base[0:P, :])
         offsets = held.tile([P, TOKENS // 16], U16, name="offsets")
         nc.sync.dma_start(offsets[:], offs)
         nc.sync.dma_start(windows[1][:], base[P : 2 * P, :])

@@ -9,13 +9,15 @@ ACT = mybir.ActivationFunctionType
 
 P = 128
 HEADS = 2
-HALF = 64
+HEAD_DIM = 128
+HALF = HEAD_DIM // 2
 TOKENS = 128
 SLOTS = 1024
-HIDDEN_BLOCKS = 2
+HIDDEN = 256
+HIDDEN_BLOCKS = HIDDEN // P
 EPS = 1e-6
 
-FLOPS = 2 * (HIDDEN_BLOCKS * P) * (HEADS * P) * TOKENS
+FLOPS = 2 * HIDDEN * (HEADS * HEAD_DIM) * TOKENS
 
 
 def tile_selfattention_s_kernel(tc, base, h, wk, k_norm_w, cs, offs, out):
@@ -26,25 +28,26 @@ def tile_selfattention_s_kernel(tc, base, h, wk, k_norm_w, cs, offs, out):
     ):
         h_sb = held.tile([P, HIDDEN_BLOCKS, TOKENS], BF16, name="h_sb")
         nc.sync.dma_start(h_sb[:], h.rearrange("(p kb) j -> p kb j", kb=HIDDEN_BLOCKS))
-        wk_sb = held.tile([P, HIDDEN_BLOCKS, HEADS * P], BF16, name="wk_sb")
+        wk_sb = held.tile([P, HIDDEN_BLOCKS, HEADS * HEAD_DIM], BF16, name="wk_sb")
         nc.scalar.dma_start(wk_sb[:], wk.rearrange("(p kb) c -> p kb c", kb=HIDDEN_BLOCKS))
 
-        windows = [held.tile([P, SLOTS], F32, name=f"window{t}") for t in range(HEADS)]
+        gain = held.tile([P, 1], F32, name="gain")
+        partner_gain = held.tile([P, 1], F32, name="partner_gain")
+        nc.sync.dma_start(gain[:], k_norm_w)
+        nc.sync.dma_start(partner_gain[0:HALF, :], k_norm_w[HALF:HEAD_DIM, :])
+        nc.sync.dma_start(partner_gain[HALF:HEAD_DIM, :], k_norm_w[0:HALF, :])
 
         cos_sin = held.tile([P, 2, TOKENS], F32, name="cos_sin")
         for half in range(2):
             nc.sync.dma_start(
                 cos_sin[half * HALF : (half + 1) * HALF, :, :], cs.rearrange("(f e) j -> e f j", e=HALF)
             )
-        gain = held.tile([P, 1], F32, name="gain")
-        partner_gain = held.tile([P, 1], F32, name="partner_gain")
-        nc.sync.dma_start(gain[:], k_norm_w)
-        nc.sync.dma_start(partner_gain[0:HALF, :], k_norm_w[HALF:P, :])
-        nc.sync.dma_start(partner_gain[HALF:P, :], k_norm_w[0:HALF, :])
-        nc.sync.dma_start(windows[0][:], base[0:P, :])
+
+        windows = [held.tile([P, SLOTS], F32, name=f"window{t}") for t in range(HEADS)]
         offsets = held.tile([P, TOKENS // 16], U16, name="offsets")
+        nc.sync.dma_start(windows[0][:], base[0:HEAD_DIM, :])
         nc.sync.dma_start(offsets[:], offs)
-        nc.sync.dma_start(windows[1][:], base[P : 2 * P, :])
+        nc.sync.dma_start(windows[1][:], base[HEAD_DIM : 2 * HEAD_DIM, :])
 
         ones = held.tile([P, P], BF16, name="ones")
         nc.vector.memset(ones[:], 1.0)
@@ -58,12 +61,12 @@ def tile_selfattention_s_kernel(tc, base, h, wk, k_norm_w, cs, offs, out):
         for t in range(HEADS):
             for kb in range(HIDDEN_BLOCKS):
                 nc.tensor.matmul(
-                    k_ps[t][:], wk_sb[:, kb, t * P : (t + 1) * P], h_sb[:, kb, :],
+                    k_ps[t][:], wk_sb[:, kb, t * HEAD_DIM : (t + 1) * HEAD_DIM], h_sb[:, kb, :],
                     start=(kb == 0), stop=(kb == HIDDEN_BLOCKS - 1),
                 )
             nc.scalar.activation(squares[t][:], k_ps[t][:], ACT.Square)
 
-        wk_partner = held.tile([P, HIDDEN_BLOCKS, HEADS * P], BF16, name="wk_partner")
+        wk_partner = held.tile([P, HIDDEN_BLOCKS, HEADS * HEAD_DIM], BF16, name="wk_partner")
         halves = wk_sb[:].rearrange("p kb (t half e) -> p (kb t) half e", half=2, e=HALF)
         partner_halves = wk_partner[:].rearrange("p kb (t half e) -> p (kb t) half e", half=2, e=HALF)
         nc.vector.tensor_copy(partner_halves[:, :, 0, :], halves[:, :, 1, :])
@@ -72,7 +75,7 @@ def tile_selfattention_s_kernel(tc, base, h, wk, k_norm_w, cs, offs, out):
         for t in range(HEADS):
             for kb in range(HIDDEN_BLOCKS):
                 nc.tensor.matmul(
-                    partner_ps[t][:], wk_partner[:, kb, t * P : (t + 1) * P], h_sb[:, kb, :],
+                    partner_ps[t][:], wk_partner[:, kb, t * HEAD_DIM : (t + 1) * HEAD_DIM], h_sb[:, kb, :],
                     start=(kb == 0), stop=(kb == HIDDEN_BLOCKS - 1),
                 )
 
@@ -91,13 +94,16 @@ def tile_selfattention_s_kernel(tc, base, h, wk, k_norm_w, cs, offs, out):
             sum_ps = psum.tile([P, TOKENS], F32, name=f"sum_ps{t}")
             nc.tensor.matmul(sum_ps[:], ones[:], squares[t][:], start=True, stop=True)
             r = held.tile([P, TOKENS], F32, name=f"r{t}")
-            nc.scalar.activation(r[:], sum_ps[:], ACT.Abs_reciprocal_sqrt, bias=eps[:, 0:1], scale=1.0 / P)
-
+            nc.scalar.activation(
+                r[:], sum_ps[:], ACT.Abs_reciprocal_sqrt, bias=eps[:, 0:1], scale=1.0 / HEAD_DIM
+            )
             nc.vector.tensor_tensor(
                 products[t][:], products[t][:], r[:].unsqueeze(1).to_broadcast([P, 2, TOKENS]), MULT
             )
+
+        for t in range(HEADS):
             nc.vector.tensor_tensor(
                 windows[t][:].indirect(offsets[:]), products[t][:, 0, :], products[t][:, 1, :], ADD
             )
             store_queue = nc.sync if t == 0 else nc.scalar
-            store_queue.dma_start(out[t * P : (t + 1) * P, :], windows[t][:])
+            store_queue.dma_start(out[t * HEAD_DIM : (t + 1) * HEAD_DIM, :], windows[t][:])

@@ -33,9 +33,9 @@ def tile_selfattention_s_kernel(tc, base, h, wk, k_norm_w, cs, offs, out):
 
         gain = held.tile([P, 1], F32, name="gain")
         partner_gain = held.tile([P, 1], F32, name="partner_gain")
-        nc.sync.dma_start(gain[:], k_norm_w)
-        nc.sync.dma_start(partner_gain[0:HALF, :], k_norm_w[HALF:HEAD_DIM, :])
-        nc.sync.dma_start(partner_gain[HALF:HEAD_DIM, :], k_norm_w[0:HALF, :])
+        nc.scalar.dma_start(gain[:], k_norm_w)
+        nc.scalar.dma_start(partner_gain[0:HALF, :], k_norm_w[HALF:HEAD_DIM, :])
+        nc.scalar.dma_start(partner_gain[HALF:HEAD_DIM, :], k_norm_w[0:HALF, :])
 
         cos_sin = held.tile([P, 2, TOKENS], F32, name="cos_sin")
         for half in range(2):
@@ -79,16 +79,13 @@ def tile_selfattention_s_kernel(tc, base, h, wk, k_norm_w, cs, offs, out):
                     start=(kb == 0), stop=(kb == HIDDEN_BLOCKS - 1),
                 )
 
-        nc.vector.tensor_scalar_mul(partner_gain[0:HALF, :], partner_gain[0:HALF, :], -1.0)
-
-        products = [held.tile([P, 2, TOKENS], F32, name=f"products{t}") for t in range(HEADS)]
+        straight = [held.tile([P, TOKENS], F32, name=f"straight{t}") for t in range(HEADS)]
+        crossed = [held.tile([P, TOKENS], F32, name=f"crossed{t}") for t in range(HEADS)]
         for t in range(HEADS):
-            nc.vector.scalar_tensor_tensor(
-                products[t][:, 0, :], k_ps[t][:], gain[:, 0:1], cos_sin[:, 0, :], MULT, MULT
-            )
-            nc.vector.scalar_tensor_tensor(
-                products[t][:, 1, :], partner_ps[t][:], partner_gain[:, 0:1], cos_sin[:, 1, :], MULT, MULT
-            )
+            nc.vector.tensor_tensor(straight[t][:], k_ps[t][:], cos_sin[:, 0, :], MULT)
+            nc.vector.tensor_tensor(crossed[t][:], partner_ps[t][:], cos_sin[:, 1, :], MULT)
+
+        nc.vector.tensor_scalar_mul(partner_gain[0:HALF, :], partner_gain[0:HALF, :], -1.0)
 
         for t in range(HEADS):
             sum_ps = psum.tile([P, TOKENS], F32, name=f"sum_ps{t}")
@@ -97,13 +94,12 @@ def tile_selfattention_s_kernel(tc, base, h, wk, k_norm_w, cs, offs, out):
             nc.scalar.activation(
                 r[:], sum_ps[:], ACT.Abs_reciprocal_sqrt, bias=eps[:, 0:1], scale=1.0 / HEAD_DIM
             )
-            nc.vector.tensor_tensor(
-                products[t][:], products[t][:], r[:].unsqueeze(1).to_broadcast([P, 2, TOKENS]), MULT
-            )
+            nc.vector.scalar_tensor_tensor(straight[t][:], straight[t][:], gain[:, 0:1], r[:], MULT, MULT)
+            nc.vector.scalar_tensor_tensor(crossed[t][:], crossed[t][:], partner_gain[:, 0:1], r[:], MULT, MULT)
 
         for t in range(HEADS):
             nc.vector.tensor_tensor(
-                windows[t][:].indirect(offsets[:]), products[t][:, 0, :], products[t][:, 1, :], ADD
+                windows[t][:].indirect(offsets[:]), straight[t][:], crossed[t][:], ADD
             )
             store_queue = nc.sync if t == 0 else nc.scalar
             store_queue.dma_start(out[t * HEAD_DIM : (t + 1) * HEAD_DIM, :], windows[t][:])

@@ -16,6 +16,8 @@ SLOTS = 1024
 HIDDEN = 256
 HIDDEN_BLOCKS = HIDDEN // P
 EPS = 1e-6
+WARM_REPEATS = 4
+WARM_MATMULS = 4
 
 FLOPS = 2 * HIDDEN * (HEADS * HEAD_DIM) * TOKENS
 
@@ -55,6 +57,12 @@ def tile_selfattention_s_kernel(tc, base, h, wk, k_norm_w, cs, offs, out):
         nc.vector.memset(eps[:], EPS)
         table_warmer = held.tile([P, 1], F32, name="table_warmer")
         nc.scalar.activation(table_warmer[:], eps[:], ACT.Abs_reciprocal_sqrt)
+
+        warm_ps = psum.tile([P, WARM_REPEATS, P], F32, name="warm_ps")
+        for warm in range(WARM_MATMULS):
+            nc.tensor.matmul(
+                warm_ps[:], ones[:], ones[:].unsqueeze(1).to_broadcast([P, WARM_REPEATS, P]), start=True, stop=True
+            )
 
         k_ps = [psum.tile([P, TOKENS], F32, name=f"k_ps{t}") for t in range(HEADS)]
         squares = [held.tile([P, TOKENS], BF16, name=f"squares{t}") for t in range(HEADS)]

@@ -17,7 +17,7 @@ HIDDEN = 256
 HIDDEN_BLOCKS = HIDDEN // P
 EPS = 1e-6
 WARM_REPEATS = 4
-WARM_MATMULS = 4
+WARM_MATMULS = 3
 
 FLOPS = 2 * HIDDEN * (HEADS * HEAD_DIM) * TOKENS
 
@@ -29,9 +29,9 @@ def tile_selfattention_s_kernel(tc, base, h, wk, k_norm_w, cs, offs, out):
         tc.psum_pool(name="psum", bufs=1) as psum,
     ):
         h_sb = held.tile([P, HIDDEN_BLOCKS, TOKENS], BF16, name="h_sb")
-        nc.sync.dma_start(h_sb[:], h.rearrange("(p kb) j -> p kb j", kb=HIDDEN_BLOCKS))
+        nc.scalar.dma_start(h_sb[:], h.rearrange("(p kb) j -> p kb j", kb=HIDDEN_BLOCKS))
         wk_sb = held.tile([P, HIDDEN_BLOCKS, HEADS * HEAD_DIM], BF16, name="wk_sb")
-        nc.scalar.dma_start(wk_sb[:], wk.rearrange("(p kb) c -> p kb c", kb=HIDDEN_BLOCKS))
+        nc.sync.dma_start(wk_sb[:], wk.rearrange("(p kb) c -> p kb c", kb=HIDDEN_BLOCKS))
 
         gain = held.tile([P, 1], F32, name="gain")
         partner_gain = held.tile([P, 1], F32, name="partner_gain")
@@ -64,6 +64,8 @@ def tile_selfattention_s_kernel(tc, base, h, wk, k_norm_w, cs, offs, out):
                 warm_ps[:], ones[:], ones[:].unsqueeze(1).to_broadcast([P, WARM_REPEATS, P]), start=True, stop=True
             )
 
+        nc.vector.tensor_scalar_mul(cos_sin[0:HALF, 1, :], cos_sin[0:HALF, 1, :], -1.0)
+
         k_ps = [psum.tile([P, TOKENS], F32, name=f"k_ps{t}") for t in range(HEADS)]
         squares = [held.tile([P, TOKENS], BF16, name=f"squares{t}") for t in range(HEADS)]
         for t in range(HEADS):
@@ -92,8 +94,6 @@ def tile_selfattention_s_kernel(tc, base, h, wk, k_norm_w, cs, offs, out):
         for t in range(HEADS):
             nc.vector.tensor_tensor(straight[t][:], k_ps[t][:], cos_sin[:, 0, :], MULT)
             nc.vector.tensor_tensor(crossed[t][:], partner_ps[t][:], cos_sin[:, 1, :], MULT)
-
-        nc.vector.tensor_scalar_mul(partner_gain[0:HALF, :], partner_gain[0:HALF, :], -1.0)
 
         for t in range(HEADS):
             sum_ps = psum.tile([P, TOKENS], F32, name=f"sum_ps{t}")

@@ -29,25 +29,26 @@ def tile_selfattention_s_kernel(tc, base, h, wk, k_norm_w, cs, offs, out):
         tc.psum_pool(name="psum", bufs=1) as psum,
     ):
         h_sb = held.tile([P, HIDDEN_BLOCKS, TOKENS], BF16, name="h_sb")
-        nc.scalar.dma_start(h_sb[:], h.rearrange("(p kb) j -> p kb j", kb=HIDDEN_BLOCKS))
+        nc.sync.dma_start(h_sb[:], h.rearrange("(p kb) j -> p kb j", kb=HIDDEN_BLOCKS))
         wk_sb = held.tile([P, HIDDEN_BLOCKS, HEADS * HEAD_DIM], BF16, name="wk_sb")
-        nc.sync.dma_start(wk_sb[:], wk.rearrange("(p kb) c -> p kb c", kb=HIDDEN_BLOCKS))
-
-        gain = held.tile([P, 1], F32, name="gain")
-        partner_gain = held.tile([P, 1], F32, name="partner_gain")
-        nc.scalar.dma_start(gain[:], k_norm_w)
-        nc.scalar.dma_start(partner_gain[0:HALF, :], k_norm_w[HALF:HEAD_DIM, :])
-        nc.scalar.dma_start(partner_gain[HALF:HEAD_DIM, :], k_norm_w[0:HALF, :])
+        nc.scalar.dma_start(wk_sb[:], wk.rearrange("(p kb) c -> p kb c", kb=HIDDEN_BLOCKS))
 
         cos_sin = held.tile([P, 2, TOKENS], F32, name="cos_sin")
-        for half in range(2):
-            nc.sync.dma_start(
+        for half, queue in enumerate((nc.sync, nc.scalar)):
+            queue.dma_start(
                 cos_sin[half * HALF : (half + 1) * HALF, :, :], cs.rearrange("(f e) j -> e f j", e=HALF)
             )
 
         windows = [held.tile([P, SLOTS], F32, name=f"window{t}") for t in range(HEADS)]
+        nc.scalar.dma_start(windows[0][:], base[0:HEAD_DIM, :])
+
+        gain = held.tile([P, 1], F32, name="gain")
+        partner_gain = held.tile([P, 1], F32, name="partner_gain")
+        nc.sync.dma_start(gain[:], k_norm_w)
+        nc.sync.dma_start(partner_gain[0:HALF, :], k_norm_w[HALF:HEAD_DIM, :])
+        nc.sync.dma_start(partner_gain[HALF:HEAD_DIM, :], k_norm_w[0:HALF, :])
+
         offsets = held.tile([P, TOKENS // 16], U16, name="offsets")
-        nc.sync.dma_start(windows[0][:], base[0:HEAD_DIM, :])
         nc.sync.dma_start(offsets[:], offs)
         nc.sync.dma_start(windows[1][:], base[HEAD_DIM : 2 * HEAD_DIM, :])
 

import concourse.mybir as mybir

F32 = mybir.dt.float32
BF16 = mybir.dt.bfloat16
U16 = mybir.dt.uint16
MULT = mybir.AluOpType.mult
ADD = mybir.AluOpType.add
ACT = mybir.ActivationFunctionType

P = 128
HEADS = 2
HEAD_DIM = 128
HALF = HEAD_DIM // 2
TOKENS = 128
SLOTS = 1024
HIDDEN = 256
HIDDEN_BLOCKS = HIDDEN // P
EPS = 1e-6
WARM_REPEATS = 4
WARM_MATMULS = 3

FLOPS = 2 * HIDDEN * (HEADS * HEAD_DIM) * TOKENS


def tile_selfattention_s_kernel(tc, base, h, wk, k_norm_w, cs, offs, out):
    nc = tc.nc
    with (
        tc.tile_pool(name="held", bufs=1) as held,
        tc.psum_pool(name="psum", bufs=1) as psum,
    ):
        h_sb = held.tile([P, HIDDEN_BLOCKS, TOKENS], BF16, name="h_sb")
        nc.sync.dma_start(h_sb[:], h.rearrange("(p kb) j -> p kb j", kb=HIDDEN_BLOCKS))
        wk_sb = held.tile([P, HIDDEN_BLOCKS, HEADS * HEAD_DIM], BF16, name="wk_sb")
        nc.scalar.dma_start(wk_sb[:], wk.rearrange("(p kb) c -> p kb c", kb=HIDDEN_BLOCKS))

        cos_sin = held.tile([P, 2, TOKENS], F32, name="cos_sin")
        for half, queue in enumerate((nc.sync, nc.scalar)):
            queue.dma_start(
                cos_sin[half * HALF : (half + 1) * HALF, :, :], cs.rearrange("(f e) j -> e f j", e=HALF)
            )

        windows = [held.tile([P, SLOTS], F32, name=f"window{t}") for t in range(HEADS)]
        nc.scalar.dma_start(windows[0][:], base[0:HEAD_DIM, :])

        gain = held.tile([P, 1], F32, name="gain")
        partner_gain = held.tile([P, 1], F32, name="partner_gain")
        nc.sync.dma_start(gain[:], k_norm_w)
        nc.sync.dma_start(partner_gain[0:HALF, :], k_norm_w[HALF:HEAD_DIM, :])
        nc.sync.dma_start(partner_gain[HALF:HEAD_DIM, :], k_norm_w[0:HALF, :])

        offsets = held.tile([P, TOKENS // 16], U16, name="offsets")
        nc.sync.dma_start(offsets[:], offs)
        nc.sync.dma_start(windows[1][:], base[HEAD_DIM : 2 * HEAD_DIM, :])

        ones = held.tile([P, P], BF16, name="ones")
        nc.vector.memset(ones[:], 1.0)
        eps = held.tile([P, 1], F32, name="eps")
        nc.vector.memset(eps[:], EPS)
        table_warmer = held.tile([P, 1], F32, name="table_warmer")
        nc.scalar.activation(table_warmer[:], eps[:], ACT.Abs_reciprocal_sqrt)

        warm_ps = psum.tile([P, WARM_REPEATS, P], F32, name="warm_ps")
        for warm in range(WARM_MATMULS):
            nc.tensor.matmul(
                warm_ps[:], ones[:], ones[:].unsqueeze(1).to_broadcast([P, WARM_REPEATS, P]), start=True, stop=True
            )

        nc.vector.tensor_scalar_mul(cos_sin[0:HALF, 1, :], cos_sin[0:HALF, 1, :], -1.0)

        k_ps = [psum.tile([P, TOKENS], F32, name=f"k_ps{t}") for t in range(HEADS)]
        squares = [held.tile([P, TOKENS], BF16, name=f"squares{t}") for t in range(HEADS)]
        for t in range(HEADS):
            for kb in range(HIDDEN_BLOCKS):
                nc.tensor.matmul(
                    k_ps[t][:], wk_sb[:, kb, t * HEAD_DIM : (t + 1) * HEAD_DIM], h_sb[:, kb, :],
                    start=(kb == 0), stop=(kb == HIDDEN_BLOCKS - 1),
                )
            nc.scalar.activation(squares[t][:], k_ps[t][:], ACT.Square)

        wk_partner = held.tile([P, HIDDEN_BLOCKS, HEADS * HEAD_DIM], BF16, name="wk_partner")
        halves = wk_sb[:].rearrange("p kb (t half e) -> p (kb t) half e", half=2, e=HALF)
        partner_halves = wk_partner[:].rearrange("p kb (t half e) -> p (kb t) half e", half=2, e=HALF)
        nc.vector.tensor_copy(partner_halves[:, :, 0, :], halves[:, :, 1, :])
        nc.vector.tensor_copy(partner_halves[:, :, 1, :], halves[:, :, 0, :])
        partner_ps = [psum.tile([P, TOKENS], F32, name=f"partner_ps{t}") for t in range(HEADS)]
        for t in range(HEADS):
            for kb in range(HIDDEN_BLOCKS):
                nc.tensor.matmul(
                    partner_ps[t][:], wk_partner[:, kb, t * HEAD_DIM : (t + 1) * HEAD_DIM], h_sb[:, kb, :],
                    start=(kb == 0), stop=(kb == HIDDEN_BLOCKS - 1),
                )

        straight = [held.tile([P, TOKENS], F32, name=f"straight{t}") for t in range(HEADS)]
        crossed = [held.tile([P, TOKENS], F32, name=f"crossed{t}") for t in range(HEADS)]
        for t in range(HEADS):
            nc.vector.tensor_tensor(straight[t][:], k_ps[t][:], cos_sin[:, 0, :], MULT)
            nc.vector.tensor_tensor(crossed[t][:], partner_ps[t][:], cos_sin[:, 1, :], MULT)

        for t in range(HEADS):
            sum_ps = psum.tile([P, TOKENS], F32, name=f"sum_ps{t}")
            nc.tensor.matmul(sum_ps[:], ones[:], squares[t][:], start=True, stop=True)
            r = held.tile([P, TOKENS], F32, name=f"r{t}")
            nc.scalar.activation(
                r[:], sum_ps[:], ACT.Abs_reciprocal_sqrt, bias=eps[:, 0:1], scale=1.0 / HEAD_DIM
            )
            nc.vector.scalar_tensor_tensor(straight[t][:], straight[t][:], gain[:, 0:1], r[:], MULT, MULT)
            nc.vector.scalar_tensor_tensor(crossed[t][:], crossed[t][:], partner_gain[:, 0:1], r[:], MULT, MULT)

        for t in range(HEADS):
            nc.vector.tensor_tensor(
                windows[t][:].indirect(offsets[:]), straight[t][:], crossed[t][:], ADD
            )
            store_queue = nc.sync if t == 0 else nc.scalar
            store_queue.dma_start(out[t * HEAD_DIM : (t + 1) * HEAD_DIM, :], windows[t][:])
